import numpy as np
import ml_dtypes

BF16 = ml_dtypes.bfloat16


def bf(x):
    return np.asarray(x, np.float32).astype(BF16)


def f32(x):
    return np.asarray(x, np.float32)


def f64(x):
    return np.asarray(x).astype(np.float64)


def striped(idx):
    return np.tile(idx.reshape(-1, 16).T, (8, 1))


V, D, M, N = 2048, 128, 512, 1024


def sigmoid(v):
    return 1.0 / (1.0 + np.exp(-v))


def setup_inputs():
    return {"table": bf(np.abs(np.random.standard_normal((V, D)))), "w_x": bf(np.random.standard_normal((D, M)) / np.sqrt(D)), "w_c": bf(np.random.standard_normal((D, M)) / np.sqrt(D)), "w_h": bf(np.random.standard_normal((D, M)) / np.sqrt(D)), "b": f32(0.3 * np.random.standard_normal((M, 1))), "ctx": bf(np.random.standard_normal((D, N))), "h0": bf(np.random.standard_normal((D, N))), "c0": f32(np.random.standard_normal((D, N))), "offs": striped(np.random.permutation(np.tile(np.arange(V), 2))[:N])}


def reference(table, w_x, w_c, w_h, b, ctx, h0, c0, offs):
    idx = offs[:16].T.reshape(-1)
    pre = f64(w_x).T @ f64(table)[idx].T + f64(w_c).T @ f64(ctx) + f64(w_h).T @ f64(h0) + f64(b)
    a_in, a_forget, a_cand, a_out = pre[:D], pre[D:2 * D], pre[2 * D:3 * D], pre[3 * D:]
    c1 = sigmoid(a_forget) * f64(c0) + sigmoid(a_in) * np.tanh(a_cand)
    return sigmoid(a_out) * np.tanh(c1)

@@ -1,0 +1,107 @@
+import concourse.mybir as mybir
+from concourse.masks import make_identity
+
+P = 128
+V = 2048
+N = 1024
+GATES = 4
+PIECE = 512
+BLOCKS = V // P
+GROUP = 4
+
+BF16, F32, U16 = mybir.dt.bfloat16, mybir.dt.float32, mybir.dt.uint16
+SIGMOID = mybir.ActivationFunctionType.Sigmoid
+TANH = mybir.ActivationFunctionType.Tanh
+GATE_FUNCTION = (SIGMOID, SIGMOID, TANH, SIGMOID)
+
+FLOPS = 2 * 3 * P * GATES * P * N
+
+
+def tile_recurrentmemory_kernel(tc, table, w_x, w_c, w_h, b, ctx, h0, c0, offs, out):
+    nc = tc.nc
+    with (
+        tc.tile_pool(name="held", bufs=1) as held,
+        tc.tile_pool(name="work", bufs=2) as work,
+        tc.psum_pool(name="psum", bufs=8) as psum,
+    ):
+        table_sb = held.tile([P, BLOCKS, P], BF16, name="table_sb")
+        table_blocks = table.rearrange("(blk p) d -> p blk d", p=P)
+        for group in range(BLOCKS // GROUP):
+            blks = slice(group * GROUP, (group + 1) * GROUP)
+            queue = nc.sync if group % 2 == 0 else nc.scalar
+            queue.dma_start(table_sb[:, blks, :], table_blocks[:, blks, :])
+        wc_sb = held.tile([P, GATES * P], BF16, name="wc_sb")
+        nc.sync.dma_start(wc_sb[:], w_c)
+        ctx_sb = held.tile([P, N], BF16, name="ctx_sb")
+        nc.scalar.dma_start(ctx_sb[:], ctx)
+        wh_sb = held.tile([P, GATES * P], BF16, name="wh_sb")
+        nc.sync.dma_start(wh_sb[:], w_h)
+        h0_sb = held.tile([P, N], BF16, name="h0_sb")
+        nc.scalar.dma_start(h0_sb[:], h0)
+        wx_sb = held.tile([P, GATES * P], BF16, name="wx_sb")
+        nc.sync.dma_start(wx_sb[:], w_x)
+        offsets = held.tile([P, N // 16], U16, name="offsets")
+        nc.sync.dma_start(offsets[:], offs)
+        bias = held.tile([P, GATES], F32, name="bias")
+        with nc.allow_non_contiguous_dma(reason="512 floats, one to a partition and gate"):
+            nc.sync.dma_start(bias[:], b.rearrange("(g r) one -> r (g one)", r=P))
+        c0_sb = held.tile([P, N], F32, name="c0_sb")
+        nc.sync.dma_start(c0_sb[:], c0)
+
+        identity = held.tile([P, P], BF16, name="identity")
+        make_identity(nc, identity[:])
+        words = held.tile([P, V], BF16, name="words")
+        for group in range(BLOCKS // GROUP):
+            flipped = psum.tile([P, GROUP * P], BF16, name="flipped", tag="bank")
+            for k in range(GROUP):
+                nc.tensor.transpose(
+                    flipped[:, k * P : (k + 1) * P], table_sb[:, group * GROUP + k, :], identity[:]
+                )
+            group_words = words[:, group * GROUP * P : (group + 1) * GROUP * P]
+            if group % 2 == 0:
+                nc.vector.tensor_copy(group_words, flipped[:])
+            else:
+                nc.scalar.copy(group_words, flipped[:])
+
+        def dense(pre, piece, g, start, stop):
+            rows = slice(g * P, (g + 1) * P)
+            cols = slice(piece * PIECE, (piece + 1) * PIECE)
+            nc.tensor.matmul(pre[:], wc_sb[:, rows], ctx_sb[:, cols], start=start, stop=False)
+            nc.tensor.matmul(pre[:], wh_sb[:, rows], h0_sb[:, cols], start=False, stop=stop)
+
+        def looked_up(pre, piece, g, start, stop):
+            rows = slice(g * P, (g + 1) * P)
+            piece_offsets = offsets[:, piece * PIECE // 16 : (piece + 1) * PIECE // 16]
+            nc.tensor.matmul(pre[:], wx_sb[:, rows], words[:].indirect(piece_offsets), start=start, stop=stop)
+
+        pre = [
+            [psum.tile([P, PIECE], F32, name=f"pre{piece}_{g}", tag="bank") for g in range(GATES)]
+            for piece in range(N // PIECE)
+        ]
+        for g in range(GATES):
+            dense(pre[0][g], 0, g, start=True, stop=False)
+        for g in range(GATES):
+            looked_up(pre[0][g], 0, g, start=False, stop=True)
+        for g in range(GATES):
+            looked_up(pre[1][g], 1, g, start=True, stop=False)
+        for g in range(GATES):
+            dense(pre[1][g], 1, g, start=False, stop=True)
+
+        for piece in range(N // PIECE):
+            cols = slice(piece * PIECE, (piece + 1) * PIECE)
+            gate = [work.tile([P, PIECE], F32, name=f"gate{g}") for g in range(GATES)]
+            for g in range(GATES):
+                nc.scalar.activation(gate[g][:], pre[piece][g][:], GATE_FUNCTION[g], bias=bias[:, g : g + 1])
+            gate_in, gate_forget, gate_cand, gate_out = gate
+
+            kept = work.tile([P, PIECE], F32, name="kept")
+            nc.vector.tensor_mul(kept[:], gate_forget[:], c0_sb[:, cols])
+            fresh = work.tile([P, PIECE], F32, name="fresh")
+            nc.vector.tensor_mul(fresh[:], gate_in[:], gate_cand[:])
+            c1 = work.tile([P, PIECE], F32, name="c1")
+            nc.vector.tensor_add(c1[:], kept[:], fresh[:])
+            tanh_c1 = work.tile([P, PIECE], F32, name="tanh_c1")
+            nc.scalar.activation(tanh_c1[:], c1[:], TANH)
+            hidden = work.tile([P, PIECE], F32, name="hidden")
+            nc.vector.tensor_mul(hidden[:], gate_out[:], tanh_c1[:])
+            nc.sync.dma_start(out[:, cols], hidden[:])

@@ -13,6 +13,8 @@ BF16, F32, U16 = mybir.dt.bfloat16, mybir.dt.float32, mybir.dt.uint16
 SIGMOID = mybir.ActivationFunctionType.Sigmoid
 TANH = mybir.ActivationFunctionType.Tanh
 GATE_FUNCTION = (SIGMOID, SIGMOID, TANH, SIGMOID)
+CELL_GATES = (0, 1, 2)
+OUT_GATE = 3
 
 FLOPS = 2 * 3 * P * GATES * P * N
 
@@ -74,34 +76,42 @@ def tile_recurrentmemory_kernel(tc, table, w_x, w_c, w_h, b, ctx, h0, c0, offs, 
             piece_offsets = offsets[:, piece * PIECE // 16 : (piece + 1) * PIECE // 16]
             nc.tensor.matmul(pre[:], wx_sb[:, rows], words[:].indirect(piece_offsets), start=start, stop=stop)
 
-        pre = [
-            [psum.tile([P, PIECE], F32, name=f"pre{piece}_{g}", tag="bank") for g in range(GATES)]
-            for piece in range(N // PIECE)
-        ]
-        for g in range(GATES):
-            dense(pre[0][g], 0, g, start=True, stop=False)
-        for g in range(GATES):
-            looked_up(pre[0][g], 0, g, start=False, stop=True)
-        for g in range(GATES):
-            looked_up(pre[1][g], 1, g, start=True, stop=False)
-        for g in range(GATES):
-            dense(pre[1][g], 1, g, start=False, stop=True)
+        pieces = range(N // PIECE)
+        pre = [[psum.tile([P, PIECE], F32, name=f"pre{piece}_{g}", tag="bank") for g in CELL_GATES] for piece in pieces]
+        for piece in pieces:
+            pre[piece].append(psum.tile([P, PIECE], F32, name=f"pre{piece}_{OUT_GATE}", tag="bank"))
+        for piece in pieces:
+            for g in CELL_GATES:
+                dense(pre[piece][g], piece, g, start=True, stop=False)
+        for piece in pieces:
+            for g in CELL_GATES:
+                looked_up(pre[piece][g], piece, g, start=False, stop=True)
+        for piece in pieces:
+            looked_up(pre[piece][OUT_GATE], piece, OUT_GATE, start=True, stop=False)
+        for piece in pieces:
+            dense(pre[piece][OUT_GATE], piece, OUT_GATE, start=False, stop=True)
 
-        for piece in range(N // PIECE):
+        def gate_of(piece, g):
+            gate = work.tile([P, PIECE], F32, name=f"gate{g}")
+            nc.scalar.activation(gate[:], pre[piece][g][:], GATE_FUNCTION[g], bias=bias[:, g : g + 1])
+            return gate
+
+        tanh_c1 = []
+        for piece in pieces:
             cols = slice(piece * PIECE, (piece + 1) * PIECE)
-            gate = [work.tile([P, PIECE], F32, name=f"gate{g}") for g in range(GATES)]
-            for g in range(GATES):
-                nc.scalar.activation(gate[g][:], pre[piece][g][:], GATE_FUNCTION[g], bias=bias[:, g : g + 1])
-            gate_in, gate_forget, gate_cand, gate_out = gate
-
+            gate_in, gate_forget, gate_cand = [gate_of(piece, g) for g in CELL_GATES]
             kept = work.tile([P, PIECE], F32, name="kept")
             nc.vector.tensor_mul(kept[:], gate_forget[:], c0_sb[:, cols])
             fresh = work.tile([P, PIECE], F32, name="fresh")
             nc.vector.tensor_mul(fresh[:], gate_in[:], gate_cand[:])
             c1 = work.tile([P, PIECE], F32, name="c1")
             nc.vector.tensor_add(c1[:], kept[:], fresh[:])
-            tanh_c1 = work.tile([P, PIECE], F32, name="tanh_c1")
-            nc.scalar.activation(tanh_c1[:], c1[:], TANH)
+            tanh_c1.append(work.tile([P, PIECE], F32, name="tanh_c1"))
+            nc.scalar.activation(tanh_c1[piece][:], c1[:], TANH)
+
+        for piece in pieces:
+            cols = slice(piece * PIECE, (piece + 1) * PIECE)
+            gate_out = gate_of(piece, OUT_GATE)
             hidden = work.tile([P, PIECE], F32, name="hidden")
-            nc.vector.tensor_mul(hidden[:], gate_out[:], tanh_c1[:])
+            nc.vector.tensor_mul(hidden[:], gate_out[:], tanh_c1[piece][:])
             nc.sync.dma_start(out[:, cols], hidden[:])

@@ -8,6 +8,7 @@ GATES = 4
 PIECE = 512
 BLOCKS = V // P
 GROUP = 4
+WARM_UP = 5
 
 BF16, F32, U16 = mybir.dt.bfloat16, mybir.dt.float32, mybir.dt.uint16
 SIGMOID = mybir.ActivationFunctionType.Sigmoid
@@ -49,6 +50,12 @@ def tile_recurrentmemory_kernel(tc, table, w_x, w_c, w_h, b, ctx, h0, c0, offs, 
             nc.sync.dma_start(bias[:], b.rearrange("(g r) one -> r (g one)", r=P))
         c0_sb = held.tile([P, N], F32, name="c0_sb")
         nc.sync.dma_start(c0_sb[:], c0)
+
+        zeros = held.tile([P, PIECE], BF16, name="zeros")
+        nc.vector.memset(zeros[:], 0.0)
+        unused = psum.tile([P, PIECE], F32, name="unused", tag="bank")
+        for warm in range(WARM_UP):
+            nc.tensor.matmul(unused[:], zeros[:, :P], zeros[:], start=True, stop=True)
 
         identity = held.tile([P, P], BF16, name="identity")
         make_identity(nc, identity[:])

@@ -4,52 +4,68 @@ from concourse.masks import make_identity
 P = 128
 V = 2048
 N = 1024
-GATES = 4
 PIECE = 512
 BLOCKS = V // P
 GROUP = 4
-WARM_UP = 5
+WARM_UP = 4
 
 BF16, F32, U16 = mybir.dt.bfloat16, mybir.dt.float32, mybir.dt.uint16
 SIGMOID = mybir.ActivationFunctionType.Sigmoid
 TANH = mybir.ActivationFunctionType.Tanh
-GATE_FUNCTION = (SIGMOID, SIGMOID, TANH, SIGMOID)
-CELL_GATES = (0, 1, 2)
-OUT_GATE = 3
 
-FLOPS = 2 * 3 * P * GATES * P * N
+IN, FORGET, CAND, OUT = range(4)
+GATE_FUNCTION = (SIGMOID, SIGMOID, TANH, SIGMOID)
+
+SUMS = ((0, IN), (0, FORGET), (0, CAND), (1, IN), (1, FORGET), (1, CAND), (0, OUT), (1, OUT))
+DENSE_FIRST = 5
+
+FLOPS = 2 * 3 * P * 4 * P * N
 
 
 def tile_recurrentmemory_kernel(tc, table, w_x, w_c, w_h, b, ctx, h0, c0, offs, out):
     nc = tc.nc
+    pieces = range(N // PIECE)
+    groups = range(BLOCKS // GROUP)
     with (
         tc.tile_pool(name="held", bufs=1) as held,
         tc.tile_pool(name="work", bufs=2) as work,
-        tc.psum_pool(name="psum", bufs=8) as psum,
+        tc.psum_pool(name="psum", bufs=5) as psum,
     ):
-        table_sb = held.tile([P, BLOCKS, P], BF16, name="table_sb")
+
+        def columns(piece):
+            return slice(piece * PIECE, (piece + 1) * PIECE)
+
+        def rows(g):
+            return slice(g * P, (g + 1) * P)
+
+        def load(queue, shape, dtype, name, source):
+            tile = held.tile(shape, dtype, name=name)
+            queue.dma_start(tile[:], source)
+            return tile
+
+        wc_sb = load(nc.sync, [P, 4 * P], BF16, "wc_sb", w_c)
+        ctx_sb = [load(nc.scalar, [P, PIECE], BF16, "ctx_sb0", ctx[:, columns(0)])]
+        wh_sb = load(nc.sync, [P, 4 * P], BF16, "wh_sb", w_h)
+        h0_sb = [load(nc.scalar, [P, PIECE], BF16, "h0_sb0", h0[:, columns(0)])]
         table_blocks = table.rearrange("(blk p) d -> p blk d", p=P)
-        for group in range(BLOCKS // GROUP):
-            blks = slice(group * GROUP, (group + 1) * GROUP)
-            queue = nc.sync if group % 2 == 0 else nc.scalar
-            queue.dma_start(table_sb[:, blks, :], table_blocks[:, blks, :])
-        wc_sb = held.tile([P, GATES * P], BF16, name="wc_sb")
-        nc.sync.dma_start(wc_sb[:], w_c)
-        ctx_sb = held.tile([P, N], BF16, name="ctx_sb")
-        nc.scalar.dma_start(ctx_sb[:], ctx)
-        wh_sb = held.tile([P, GATES * P], BF16, name="wh_sb")
-        nc.sync.dma_start(wh_sb[:], w_h)
-        h0_sb = held.tile([P, N], BF16, name="h0_sb")
-        nc.scalar.dma_start(h0_sb[:], h0)
-        wx_sb = held.tile([P, GATES * P], BF16, name="wx_sb")
-        nc.sync.dma_start(wx_sb[:], w_x)
+        table_sb = [
+            load(
+                nc.sync if group % 2 == 0 else nc.scalar,
+                [P, GROUP, P],
+                BF16,
+                f"table_sb{group}",
+                table_blocks[:, group * GROUP : (group + 1) * GROUP, :],
+            )
+            for group in groups
+        ]
+        ctx_sb.append(load(nc.sync, [P, PIECE], BF16, "ctx_sb1", ctx[:, columns(1)]))
+        h0_sb.append(load(nc.sync, [P, PIECE], BF16, "h0_sb1", h0[:, columns(1)]))
+        wx_sb = load(nc.sync, [P, 4 * P], BF16, "wx_sb", w_x)
         offsets = held.tile([P, N // 16], U16, name="offsets")
         nc.sync.dma_start(offsets[:], offs)
-        bias = held.tile([P, GATES], F32, name="bias")
         with nc.allow_non_contiguous_dma(reason="512 floats, one to a partition and gate"):
-            nc.sync.dma_start(bias[:], b.rearrange("(g r) one -> r (g one)", r=P))
-        c0_sb = held.tile([P, N], F32, name="c0_sb")
-        nc.sync.dma_start(c0_sb[:], c0)
+            bias = load(nc.sync, [P, 4], F32, "bias", b.rearrange("(g r) one -> r (g one)", r=P))
+        c0_sb = [load(nc.sync, [P, PIECE], F32, f"c0_sb{piece}", c0[:, columns(piece)]) for piece in pieces]
 
         zeros = held.tile([P, PIECE], BF16, name="zeros")
         nc.vector.memset(zeros[:], 0.0)
@@ -57,58 +73,62 @@ def tile_recurrentmemory_kernel(tc, table, w_x, w_c, w_h, b, ctx, h0, c0, offs, 
         for warm in range(WARM_UP):
             nc.tensor.matmul(unused[:], zeros[:, :P], zeros[:], start=True, stop=True)
 
+        pre = {}
+
+        def dense(sums, opens):
+            for weights, moving, is_first in ((wc_sb, ctx_sb, True), (wh_sb, h0_sb, False)):
+                for piece, g in sums:
+                    nc.tensor.matmul(
+                        pre[piece, g][:],
+                        weights[:, rows(g)],
+                        moving[piece][:],
+                        start=opens and is_first,
+                        stop=not opens and not is_first,
+                    )
+
+        for piece, g in SUMS[:3]:
+            pre[piece, g] = psum.tile([P, PIECE], F32, name=f"pre{piece}_{g}", tag="first_sums", bufs=3)
+        dense(SUMS[:3], opens=True)
+
         identity = held.tile([P, P], BF16, name="identity")
         make_identity(nc, identity[:])
         words = held.tile([P, V], BF16, name="words")
-        for group in range(BLOCKS // GROUP):
+        for group in groups:
             flipped = psum.tile([P, GROUP * P], BF16, name="flipped", tag="bank")
             for k in range(GROUP):
-                nc.tensor.transpose(
-                    flipped[:, k * P : (k + 1) * P], table_sb[:, group * GROUP + k, :], identity[:]
-                )
+                nc.tensor.transpose(flipped[:, k * P : (k + 1) * P], table_sb[group][:, k, :], identity[:])
             group_words = words[:, group * GROUP * P : (group + 1) * GROUP * P]
             if group % 2 == 0:
                 nc.vector.tensor_copy(group_words, flipped[:])
             else:
                 nc.scalar.copy(group_words, flipped[:])
 
-        def dense(pre, piece, g, start, stop):
-            rows = slice(g * P, (g + 1) * P)
-            cols = slice(piece * PIECE, (piece + 1) * PIECE)
-            nc.tensor.matmul(pre[:], wc_sb[:, rows], ctx_sb[:, cols], start=start, stop=False)
-            nc.tensor.matmul(pre[:], wh_sb[:, rows], h0_sb[:, cols], start=False, stop=stop)
+        for piece, g in SUMS[3:]:
+            pre[piece, g] = psum.tile([P, PIECE], F32, name=f"pre{piece}_{g}", tag="bank")
+        dense(SUMS[3:DENSE_FIRST], opens=True)
 
-        def looked_up(pre, piece, g, start, stop):
-            rows = slice(g * P, (g + 1) * P)
+        for count, (piece, g) in enumerate(SUMS):
             piece_offsets = offsets[:, piece * PIECE // 16 : (piece + 1) * PIECE // 16]
-            nc.tensor.matmul(pre[:], wx_sb[:, rows], words[:].indirect(piece_offsets), start=start, stop=stop)
-
-        pieces = range(N // PIECE)
-        pre = [[psum.tile([P, PIECE], F32, name=f"pre{piece}_{g}", tag="bank") for g in CELL_GATES] for piece in pieces]
-        for piece in pieces:
-            pre[piece].append(psum.tile([P, PIECE], F32, name=f"pre{piece}_{OUT_GATE}", tag="bank"))
-        for piece in pieces:
-            for g in CELL_GATES:
-                dense(pre[piece][g], piece, g, start=True, stop=False)
-        for piece in pieces:
-            for g in CELL_GATES:
-                looked_up(pre[piece][g], piece, g, start=False, stop=True)
-        for piece in pieces:
-            looked_up(pre[piece][OUT_GATE], piece, OUT_GATE, start=True, stop=False)
-        for piece in pieces:
-            dense(pre[piece][OUT_GATE], piece, OUT_GATE, start=False, stop=True)
+            nc.tensor.matmul(
+                pre[piece, g][:],
+                wx_sb[:, rows(g)],
+                words[:].indirect(piece_offsets),
+                start=count >= DENSE_FIRST,
+                stop=count < DENSE_FIRST,
+            )
+        for one_sum in SUMS[DENSE_FIRST:]:
+            dense([one_sum], opens=False)
 
         def gate_of(piece, g):
             gate = work.tile([P, PIECE], F32, name=f"gate{g}")
-            nc.scalar.activation(gate[:], pre[piece][g][:], GATE_FUNCTION[g], bias=bias[:, g : g + 1])
+            nc.scalar.activation(gate[:], pre[piece, g][:], GATE_FUNCTION[g], bias=bias[:, g : g + 1])
             return gate
 
         tanh_c1 = []
         for piece in pieces:
-            cols = slice(piece * PIECE, (piece + 1) * PIECE)
-            gate_in, gate_forget, gate_cand = [gate_of(piece, g) for g in CELL_GATES]
+            gate_in, gate_forget, gate_cand = [gate_of(piece, g) for g in (IN, FORGET, CAND)]
             kept = work.tile([P, PIECE], F32, name="kept")
-            nc.vector.tensor_mul(kept[:], gate_forget[:], c0_sb[:, cols])
+            nc.vector.tensor_mul(kept[:], gate_forget[:], c0_sb[piece][:])
             fresh = work.tile([P, PIECE], F32, name="fresh")
             nc.vector.tensor_mul(fresh[:], gate_in[:], gate_cand[:])
             c1 = work.tile([P, PIECE], F32, name="c1")
@@ -117,8 +137,7 @@ def tile_recurrentmemory_kernel(tc, table, w_x, w_c, w_h, b, ctx, h0, c0, offs, 
             nc.scalar.activation(tanh_c1[piece][:], c1[:], TANH)
 
         for piece in pieces:
-            cols = slice(piece * PIECE, (piece + 1) * PIECE)
-            gate_out = gate_of(piece, OUT_GATE)
+            gate_out = gate_of(piece, OUT)
             hidden = work.tile([P, PIECE], F32, name="hidden")
             nc.vector.tensor_mul(hidden[:], gate_out[:], tanh_c1[piece][:])
-            nc.sync.dma_start(out[:, cols], hidden[:])
+            nc.sync.dma_start(out[:, columns(piece)], hidden[:])

@@ -47,6 +47,8 @@ def tile_recurrentmemory_kernel(tc, table, w_x, w_c, w_h, b, ctx, h0, c0, offs, 
         ctx_sb = [load(nc.scalar, [P, PIECE], BF16, "ctx_sb0", ctx[:, columns(0)])]
         wh_sb = load(nc.sync, [P, 4 * P], BF16, "wh_sb", w_h)
         h0_sb = [load(nc.scalar, [P, PIECE], BF16, "h0_sb0", h0[:, columns(0)])]
+        with nc.allow_non_contiguous_dma(reason="512 floats, one to a partition and gate"):
+            bias = load(nc.sync, [P, 4], F32, "bias", b.rearrange("(g r) one -> r (g one)", r=P))
         table_blocks = table.rearrange("(blk p) d -> p blk d", p=P)
         table_sb = [
             load(
@@ -63,8 +65,6 @@ def tile_recurrentmemory_kernel(tc, table, w_x, w_c, w_h, b, ctx, h0, c0, offs, 
         wx_sb = load(nc.sync, [P, 4 * P], BF16, "wx_sb", w_x)
         offsets = held.tile([P, N // 16], U16, name="offsets")
         nc.sync.dma_start(offsets[:], offs)
-        with nc.allow_non_contiguous_dma(reason="512 floats, one to a partition and gate"):
-            bias = load(nc.sync, [P, 4], F32, "bias", b.rearrange("(g r) one -> r (g one)", r=P))
         c0_sb = [load(nc.sync, [P, PIECE], F32, f"c0_sb{piece}", c0[:, columns(piece)]) for piece in pieces]
 
         zeros = held.tile([P, PIECE], BF16, name="zeros")
@@ -97,11 +97,7 @@ def tile_recurrentmemory_kernel(tc, table, w_x, w_c, w_h, b, ctx, h0, c0, offs, 
             flipped = psum.tile([P, GROUP * P], BF16, name="flipped", tag="bank")
             for k in range(GROUP):
                 nc.tensor.transpose(flipped[:, k * P : (k + 1) * P], table_sb[group][:, k, :], identity[:])
-            group_words = words[:, group * GROUP * P : (group + 1) * GROUP * P]
-            if group % 2 == 0:
-                nc.vector.tensor_copy(group_words, flipped[:])
-            else:
-                nc.scalar.copy(group_words, flipped[:])
+            nc.vector.tensor_copy(words[:, group * GROUP * P : (group + 1) * GROUP * P], flipped[:])
 
         for piece, g in SUMS[3:]:
             pre[piece, g] = psum.tile([P, PIECE], F32, name=f"pre{piece}_{g}", tag="bank")

@@ -47,8 +47,6 @@ def tile_recurrentmemory_kernel(tc, table, w_x, w_c, w_h, b, ctx, h0, c0, offs, 
         ctx_sb = [load(nc.scalar, [P, PIECE], BF16, "ctx_sb0", ctx[:, columns(0)])]
         wh_sb = load(nc.sync, [P, 4 * P], BF16, "wh_sb", w_h)
         h0_sb = [load(nc.scalar, [P, PIECE], BF16, "h0_sb0", h0[:, columns(0)])]
-        with nc.allow_non_contiguous_dma(reason="512 floats, one to a partition and gate"):
-            bias = load(nc.sync, [P, 4], F32, "bias", b.rearrange("(g r) one -> r (g one)", r=P))
         table_blocks = table.rearrange("(blk p) d -> p blk d", p=P)
         table_sb = [
             load(
@@ -60,6 +58,7 @@ def tile_recurrentmemory_kernel(tc, table, w_x, w_c, w_h, b, ctx, h0, c0, offs, 
             )
             for group in groups
         ]
+        b_rows = load(nc.sync, [4, P], F32, "b_rows", b.rearrange("(g r) one -> g (r one)", r=P))
         ctx_sb.append(load(nc.sync, [P, PIECE], BF16, "ctx_sb1", ctx[:, columns(1)]))
         h0_sb.append(load(nc.sync, [P, PIECE], BF16, "h0_sb1", h0[:, columns(1)]))
         wx_sb = load(nc.sync, [P, 4 * P], BF16, "wx_sb", w_x)
@@ -98,6 +97,13 @@ def tile_recurrentmemory_kernel(tc, table, w_x, w_c, w_h, b, ctx, h0, c0, offs, 
             for k in range(GROUP):
                 nc.tensor.transpose(flipped[:, k * P : (k + 1) * P], table_sb[group][:, k, :], identity[:])
             nc.vector.tensor_copy(words[:, group * GROUP * P : (group + 1) * GROUP * P], flipped[:])
+
+        identity4 = held.tile([4, 4], F32, name="identity4")
+        make_identity(nc, identity4[:])
+        bias_psum = psum.tile([P, 4], F32, name="bias_psum", tag="bank")
+        nc.tensor.matmul(bias_psum[:], b_rows[:], identity4[:], start=True, stop=True)
+        bias = held.tile([P, 4], F32, name="bias")
+        nc.vector.tensor_copy(bias[:], bias_psum[:])
 
         for piece, g in SUMS[3:]:
             pre[piece, g] = psum.tile([P, PIECE], F32, name=f"pre{piece}_{g}", tag="bank")

@@ -17,7 +17,7 @@ IN, FORGET, CAND, OUT = range(4)
 GATE_FUNCTION = (SIGMOID, SIGMOID, TANH, SIGMOID)
 
 SUMS = ((0, IN), (0, FORGET), (0, CAND), (1, IN), (1, FORGET), (1, CAND), (0, OUT), (1, OUT))
-DENSE_FIRST = 5
+DENSE_FIRST = 6
 
 FLOPS = 2 * 3 * P * 4 * P * N
 
@@ -58,12 +58,13 @@ def tile_recurrentmemory_kernel(tc, table, w_x, w_c, w_h, b, ctx, h0, c0, offs, 
             )
             for group in groups
         ]
-        b_rows = load(nc.sync, [4, P], F32, "b_rows", b.rearrange("(g r) one -> g (r one)", r=P))
         ctx_sb.append(load(nc.sync, [P, PIECE], BF16, "ctx_sb1", ctx[:, columns(1)]))
         h0_sb.append(load(nc.sync, [P, PIECE], BF16, "h0_sb1", h0[:, columns(1)]))
         wx_sb = load(nc.sync, [P, 4 * P], BF16, "wx_sb", w_x)
         offsets = held.tile([P, N // 16], U16, name="offsets")
         nc.sync.dma_start(offsets[:], offs)
+        with nc.allow_non_contiguous_dma(reason="512 floats, one to a partition and gate"):
+            bias = load(nc.sync, [P, 4], F32, "bias", b.rearrange("(g r) one -> r (g one)", r=P))
         c0_sb = [load(nc.sync, [P, PIECE], F32, f"c0_sb{piece}", c0[:, columns(piece)]) for piece in pieces]
 
         zeros = held.tile([P, PIECE], BF16, name="zeros")
@@ -71,6 +72,9 @@ def tile_recurrentmemory_kernel(tc, table, w_x, w_c, w_h, b, ctx, h0, c0, offs, 
         unused = psum.tile([P, PIECE], F32, name="unused", tag="bank")
         for warm in range(WARM_UP):
             nc.tensor.matmul(unused[:], zeros[:, :P], zeros[:], start=True, stop=True)
+
+        early = held.tile([P, 1], F32, name="early")
+        nc.scalar.activation(early[:], zeros[:, :1], SIGMOID)
 
         pre = {}
 
@@ -96,14 +100,11 @@ def tile_recurrentmemory_kernel(tc, table, w_x, w_c, w_h, b, ctx, h0, c0, offs, 
             flipped = psum.tile([P, GROUP * P], BF16, name="flipped", tag="bank")
             for k in range(GROUP):
                 nc.tensor.transpose(flipped[:, k * P : (k + 1) * P], table_sb[group][:, k, :], identity[:])
-            nc.vector.tensor_copy(words[:, group * GROUP * P : (group + 1) * GROUP * P], flipped[:])
-
-        identity4 = held.tile([4, 4], F32, name="identity4")
-        make_identity(nc, identity4[:])
-        bias_psum = psum.tile([P, 4], F32, name="bias_psum", tag="bank")
-        nc.tensor.matmul(bias_psum[:], b_rows[:], identity4[:], start=True, stop=True)
-        bias = held.tile([P, 4], F32, name="bias")
-        nc.vector.tensor_copy(bias[:], bias_psum[:])
+            group_words = words[:, group * GROUP * P : (group + 1) * GROUP * P]
+            if group % 2 == 0:
+                nc.vector.tensor_copy(group_words, flipped[:])
+            else:
+                nc.scalar.copy(group_words, flipped[:])
 
         for piece, g in SUMS[3:]:
             pre[piece, g] = psum.tile([P, PIECE], F32, name=f"pre{piece}_{g}", tag="bank")

import concourse.mybir as mybir
from concourse.masks import make_identity

P = 128
V = 2048
N = 1024
PIECE = 512
BLOCKS = V // P
GROUP = 4
WARM_UP = 4

BF16, F32, U16 = mybir.dt.bfloat16, mybir.dt.float32, mybir.dt.uint16
SIGMOID = mybir.ActivationFunctionType.Sigmoid
TANH = mybir.ActivationFunctionType.Tanh

IN, FORGET, CAND, OUT = range(4)
GATE_FUNCTION = (SIGMOID, SIGMOID, TANH, SIGMOID)

SUMS = ((0, IN), (0, FORGET), (0, CAND), (1, IN), (1, FORGET), (1, CAND), (0, OUT), (1, OUT))
DENSE_FIRST = 6

FLOPS = 2 * 3 * P * 4 * P * N


def tile_recurrentmemory_kernel(tc, table, w_x, w_c, w_h, b, ctx, h0, c0, offs, out):
    nc = tc.nc
    pieces = range(N // PIECE)
    groups = range(BLOCKS // GROUP)
    with (
        tc.tile_pool(name="held", bufs=1) as held,
        tc.tile_pool(name="work", bufs=2) as work,
        tc.psum_pool(name="psum", bufs=5) as psum,
    ):

        def columns(piece):
            return slice(piece * PIECE, (piece + 1) * PIECE)

        def rows(g):
            return slice(g * P, (g + 1) * P)

        def load(queue, shape, dtype, name, source):
            tile = held.tile(shape, dtype, name=name)
            queue.dma_start(tile[:], source)
            return tile

        wc_sb = load(nc.sync, [P, 4 * P], BF16, "wc_sb", w_c)
        ctx_sb = [load(nc.scalar, [P, PIECE], BF16, "ctx_sb0", ctx[:, columns(0)])]
        wh_sb = load(nc.sync, [P, 4 * P], BF16, "wh_sb", w_h)
        h0_sb = [load(nc.scalar, [P, PIECE], BF16, "h0_sb0", h0[:, columns(0)])]
        table_blocks = table.rearrange("(blk p) d -> p blk d", p=P)
        table_sb = [
            load(
                nc.sync if group % 2 == 0 else nc.scalar,
                [P, GROUP, P],
                BF16,
                f"table_sb{group}",
                table_blocks[:, group * GROUP : (group + 1) * GROUP, :],
            )
            for group in groups
        ]
        ctx_sb.append(load(nc.sync, [P, PIECE], BF16, "ctx_sb1", ctx[:, columns(1)]))
        h0_sb.append(load(nc.sync, [P, PIECE], BF16, "h0_sb1", h0[:, columns(1)]))
        wx_sb = load(nc.sync, [P, 4 * P], BF16, "wx_sb", w_x)
        offsets = held.tile([P, N // 16], U16, name="offsets")
        nc.sync.dma_start(offsets[:], offs)
        with nc.allow_non_contiguous_dma(reason="512 floats, one to a partition and gate"):
            bias = load(nc.sync, [P, 4], F32, "bias", b.rearrange("(g r) one -> r (g one)", r=P))
        c0_sb = [load(nc.sync, [P, PIECE], F32, f"c0_sb{piece}", c0[:, columns(piece)]) for piece in pieces]

        zeros = held.tile([P, PIECE], BF16, name="zeros")
        nc.vector.memset(zeros[:], 0.0)
        unused = psum.tile([P, PIECE], F32, name="unused", tag="bank")
        for warm in range(WARM_UP):
            nc.tensor.matmul(unused[:], zeros[:, :P], zeros[:], start=True, stop=True)

        early = held.tile([P, 1], F32, name="early")
        nc.scalar.activation(early[:], zeros[:, :1], SIGMOID)

        pre = {}

        def dense(sums, opens):
            for weights, moving, is_first in ((wc_sb, ctx_sb, True), (wh_sb, h0_sb, False)):
                for piece, g in sums:
                    nc.tensor.matmul(
                        pre[piece, g][:],
                        weights[:, rows(g)],
                        moving[piece][:],
                        start=opens and is_first,
                        stop=not opens and not is_first,
                    )

        for piece, g in SUMS[:3]:
            pre[piece, g] = psum.tile([P, PIECE], F32, name=f"pre{piece}_{g}", tag="first_sums", bufs=3)
        dense(SUMS[:3], opens=True)

        identity = held.tile([P, P], BF16, name="identity")
        make_identity(nc, identity[:])
        words = held.tile([P, V], BF16, name="words")
        for group in groups:
            flipped = psum.tile([P, GROUP * P], BF16, name="flipped", tag="bank")
            for k in range(GROUP):
                nc.tensor.transpose(flipped[:, k * P : (k + 1) * P], table_sb[group][:, k, :], identity[:])
            group_words = words[:, group * GROUP * P : (group + 1) * GROUP * P]
            if group % 2 == 0:
                nc.vector.tensor_copy(group_words, flipped[:])
            else:
                nc.scalar.copy(group_words, flipped[:])

        for piece, g in SUMS[3:]:
            pre[piece, g] = psum.tile([P, PIECE], F32, name=f"pre{piece}_{g}", tag="bank")
        dense(SUMS[3:DENSE_FIRST], opens=True)

        for count, (piece, g) in enumerate(SUMS):
            piece_offsets = offsets[:, piece * PIECE // 16 : (piece + 1) * PIECE // 16]
            nc.tensor.matmul(
                pre[piece, g][:],
                wx_sb[:, rows(g)],
                words[:].indirect(piece_offsets),
                start=count >= DENSE_FIRST,
                stop=count < DENSE_FIRST,
            )
        for one_sum in SUMS[DENSE_FIRST:]:
            dense([one_sum], opens=False)

        def gate_of(piece, g):
            gate = work.tile([P, PIECE], F32, name=f"gate{g}")
            nc.scalar.activation(gate[:], pre[piece, g][:], GATE_FUNCTION[g], bias=bias[:, g : g + 1])
            return gate

        tanh_c1 = []
        for piece in pieces:
            gate_in, gate_forget, gate_cand = [gate_of(piece, g) for g in (IN, FORGET, CAND)]
            kept = work.tile([P, PIECE], F32, name="kept")
            nc.vector.tensor_mul(kept[:], gate_forget[:], c0_sb[piece][:])
            fresh = work.tile([P, PIECE], F32, name="fresh")
            nc.vector.tensor_mul(fresh[:], gate_in[:], gate_cand[:])
            c1 = work.tile([P, PIECE], F32, name="c1")
            nc.vector.tensor_add(c1[:], kept[:], fresh[:])
            tanh_c1.append(work.tile([P, PIECE], F32, name="tanh_c1"))
            nc.scalar.activation(tanh_c1[piece][:], c1[:], TANH)

        for piece in pieces:
            gate_out = gate_of(piece, OUT)
            hidden = work.tile([P, PIECE], F32, name="hidden")
            nc.vector.tensor_mul(hidden[:], gate_out[:], tanh_c1[piece][:])
            nc.sync.dma_start(out[:, columns(piece)], hidden[:])
